import numpy as np
import ml_dtypes


def mxq(x, axis, fmt="e4m3"):
    dtype, down = {"e4m3": (ml_dtypes.float8_e4m3fn, 7), "e5m2": (ml_dtypes.float8_e5m2, 14)}[fmt]
    v = np.moveaxis(np.asarray(x, np.float32).astype(ml_dtypes.bfloat16).astype(np.float64), axis, -1)
    blocks = v.reshape(v.shape[:-1] + (-1, 32))
    amax = np.abs(blocks).max(-1, keepdims=True)
    byte = np.maximum(np.where(amax > 0, np.frexp(amax)[1] - 1 + 127, 0) - down, 1)
    scale = np.exp2(byte - 127.0)
    codes = (blocks / scale).astype(np.float32).astype(dtype).astype(np.float64)
    return np.moveaxis((codes * scale).reshape(v.shape), -1, axis)


WIDE = False


def mx_kscale(k):
    if not WIDE:
        return np.ones(k)
    levels = np.array([10, -10, 5, -5, 0])
    if k % 512:
        return np.exp2(np.random.permutation(np.resize(levels, k // 32))).repeat(32)
    a = np.empty((k // 512, 16))
    for p in range(k // 512):
        a[p, :8] = np.random.permutation(np.resize(levels, 8))
        for g in range(8):
            far = levels[np.abs(levels - a[p, g]) >= 10]
            a[p, g + 8] = far[np.random.randint(len(far))]
    return np.exp2(a.ravel()).repeat(32)


BF16 = ml_dtypes.bfloat16


def bf(x):
    return np.asarray(x, np.float32).astype(BF16)


def f64(x):
    return np.asarray(x).astype(np.float64)


C, S, L, D, NK = 16, 1024, 3, 32, 96
K = NK // L


def convs(Ec, Ws, bs):
    E = np.transpose(Ec, (1, 0, 2, 3))
    res = []
    for h in range(1, L + 1):
        P = L - h + 1
        win = np.stack([E[:, :, p:p + h, :] for p in range(P)], axis=0).reshape(P * S, C * h * D)
        z = win @ Ws[h - 1].reshape(K * C, C * h * D).T + bs[h - 1].reshape(1, K * C)
        res.append(z.reshape(P, S, K, C))
    return res


def setup_inputs():
    s = mx_kscale(S)
    u = mx_kscale(K * C).reshape(K, C)
    Ec0 = bf(np.random.standard_normal((C, S, L, D)))
    W0 = [bf(np.random.standard_normal((K, C, C, h, D)) / np.sqrt(C * h * D)) for h in range(1, L + 1)]
    bs = [bf(np.random.standard_normal((K, C)) * 0.3) for h in range(1, L + 1)]
    ug = np.repeat(u.T, L, axis=1)
    g = np.random.standard_normal((C, S, 1, NK)) * np.exp2(np.random.randint(-6, 1, (1, S, 1, 1))) * 2.0
    g = bf(g * ug[:, None, None, :] / s[None, :, None, None])
    zs = convs(f64(Ec0), [f64(w) for w in W0], [f64(b) for b in bs])
    inp = {'Ec': bf(f64(Ec0) * s[None, :, None, None])}
    for h in range(1, L + 1):
        inp['W%d' % h] = bf(f64(W0[h - 1]) / u[:, :, None, None, None])
    for h in range(1, L + 1):
        inp['b%d' % h] = bs[h - 1]
    for h in range(1, L + 1):
        inp['conv%d' % h] = np.asarray(zs[h - 1], np.float32)
    inp['grad_out'] = g
    return inp


def reference(Ec, W1, W2, W3, b1, b2, b3, conv1, conv2, conv3, grad_out):
    g = f64(grad_out)[:, :, 0, :]
    Ws = [f64(W1), f64(W2), f64(W3)]
    zs = [f64(conv1), f64(conv2), f64(conv3)]
    acc = np.zeros((S, C, L, D))
    dzs = []
    for h in range(1, L + 1):
        P = L - h + 1
        z = zs[h - 1]
        gh = np.transpose(g[:, :, h - 1::L], (1, 2, 0))
        m = np.max(z, axis=0)
        hit = (z == m[None]) * 1.0
        n = np.sum(hit, axis=0)
        dz = gh[None] * hit * (((m > 0.0) * 1.0) / n)[None]
        dzs.append(dz)
        d = mxq(dz.reshape(P * S, K * C), 1, 'e5m2') @ mxq(Ws[h - 1].reshape(K * C, C * h * D), 0, 'e4m3')
        d = d.reshape(P, S, C, h, D)
        for p in range(P):
            acc[:, :, p:p + h, :] = acc[:, :, p:p + h, :] + d[p]
    dEc = np.transpose(acc, (1, 0, 2, 3))
    dz3 = dzs[2].reshape(S, K * C)
    E = np.transpose(f64(Ec), (1, 0, 2, 3)).reshape(S, C * L * D)
    dw3 = mxq(dz3, 0, 'e5m2').T @ mxq(E, 0, 'e4m3')
    return dEc, dw3.reshape(K, C, C, L, D)

@@ -1,0 +1,378 @@
+from contextlib import ExitStack
+
+import concourse.mybir as mybir
+from concourse.masks import make_identity
+
+FLOPS = 6979321856
+
+F32 = mybir.dt.float32
+BF16 = mybir.dt.bfloat16
+U32 = mybir.dt.uint32
+U8 = mybir.dt.uint8
+E4M3 = mybir.dt.float8_e4m3fn_x4
+E5M2 = mybir.dt.float8_e5m2_x4
+ALU = mybir.AluOpType
+
+P = 128
+TINY = 1e-45
+THIRD = 1.0 / 3.0
+
+
+def tile_vrtconv_t_v_kernel(tc, Ec, W1, W2, W3, b1, b2, b3, conv1, conv2, conv3, grad_out, out_0, out_1):
+    nc = tc.nc
+
+    g_v = grad_out.rearrange("o (g p j) x i -> g p o (j x i)", g=2, p=P, j=4)
+    e_v = Ec.rearrange("c (g p j) l d -> g p c (j l d)", g=2, p=P, j=4)
+    z1_v = conv1.rearrange("q (g p j) k o -> g p q (j k o)", g=2, p=P, j=4)
+    z2_v = conv2.rearrange("q (g p j) k o -> g p q (j k o)", g=2, p=P, j=4)
+    z3_v = conv3.rearrange("q (g p j) k o -> g p (q j k o)", g=2, p=P, j=4)
+    w1_v = W1.rearrange("k o c a d -> (k o) (c a d)").rearrange("(p t) w -> p t w", t=4)
+    w2_v = W2.rearrange("k o c a d -> (k o) (c a d)").rearrange("(p t) w -> p t w", t=4)
+    w3_v = W3.rearrange("k o c a d -> (k o) (c a d)").rearrange("(p t) w -> p t w", t=4)
+    o0_v = out_0.rearrange("c (g p j) l d -> g p c (j l d)", g=2, p=P, j=4)
+    o1_v = out_1.rearrange("k o c a d -> (k o) (c a d)").rearrange("(m p) w -> p m w", p=P)
+
+    with ExitStack() as ctx:
+        sb = ctx.enter_context(tc.tile_pool(name="sb", bufs=1))
+        ps = ctx.enter_context(tc.psum_pool(name="ps", bufs=1))
+
+        wc = sb.tile([P, 6, 512], U32, name="wc", tag="wc", align_bytes=64)
+        ws = sb.tile([P, 6, 512], U8, name="ws", tag="ws", align_bytes=64)
+        ec = sb.tile([P, 2, 1536], U32, name="ec", tag="ec", align_bytes=64)
+        es = sb.tile([P, 2, 1536], U8, name="es", tag="es", align_bytes=64)
+        d3c = sb.tile([P, 2, 512], U32, name="d3c", tag="d3c", align_bytes=64)
+        d3s = sb.tile([P, 2, 512], U8, name="d3s", tag="d3s", align_bytes=64)
+        t3c = sb.tile([P, 2, 512], U32, name="t3c", tag="t3c", align_bytes=64)
+        t3s = sb.tile([P, 2, 512], U8, name="t3s", tag="t3s", align_bytes=64)
+
+        def load_g(g):
+            graw = sb.tile([P, 16, 384], BF16, name="graw", tag="graw")
+            nc.sync.dma_start(out=graw[:], in_=g_v[g])
+            return graw
+
+        def load_z3(g):
+            z3 = sb.tile([P, 4, 512], F32, name="z3", tag="z3")
+            nc.sync.dma_start(out=z3[:].rearrange("p j f -> p (j f)"), in_=z3_v[g])
+            return z3
+
+        def unit_tiles():
+            z1 = sb.tile([P, 3, 1024], F32, name="z1", tag="z1", bufs=2)
+            z2 = sb.tile([P, 2, 1024], F32, name="z2", tag="z2", bufs=2)
+            return z1, z2
+
+        def load_part(zz, u, lo, hi):
+            g, jp = divmod(u, 2)
+            nc.sync.dma_start(out=zz[0][:, :, lo:hi], in_=z1_v[g][:, :, 1024 * jp + lo:1024 * jp + hi])
+            nc.sync.dma_start(out=zz[1][:, :, lo:hi], in_=z2_v[g][:, :, 1024 * jp + lo:1024 * jp + hi])
+
+        def reorder_g(graw, j, eng):
+            gr = sb.tile([P, 512, 3], BF16, name="gr", tag="gr", bufs=4)
+            dst = gr[:].rearrange("p (k o) h -> p k o h", o=16)
+            src = graw[:, :, 96 * j:96 * (j + 1)].rearrange("p o (k h) -> p k o h", h=3)
+            if eng == 0:
+                nc.vector.tensor_copy(out=dst, in_=src)
+            else:
+                nc.scalar.copy(out=dst, in_=src)
+            return gr
+
+        def il_tile():
+            il = sb.tile([P, 512, 4], BF16, name="il", tag="il", bufs=2, align_bytes=64)
+            return il
+
+        def w_interleave(src):
+            il = il_tile()
+            nc.scalar.copy(out=il[:].rearrange("p (c d) t -> p c d t", d=32), in_=src)
+            return il
+
+        def w_quantize(b, il):
+            nc.vector.quantize_mx(
+                out=wc[:, b, :].bitcast(E4M3), scales=ws[:, b, :], in_=il[:].rearrange("p c t -> p (c t)")
+            )
+
+        def e_load(g):
+            eraw = sb.tile([P, 16, 384], BF16, name="eraw", tag="big", bufs=2, align_bytes=64)
+            nc.sync.dma_start(out=eraw[:], in_=e_v[g])
+            return eraw
+
+        def e_interleave(eraw):
+            ei = sb.tile([P, 1536, 4], BF16, name="ei", tag="big", bufs=2, align_bytes=64)
+            for i in range(4):
+                nc.scalar.copy(
+                    out=ei[:, 384 * i:384 * (i + 1), :].rearrange("p (c w) t -> p c w t", w=96),
+                    in_=eraw[:, 4 * i:4 * i + 4, :].rearrange("p c (t w) -> p c w t", t=4),
+                )
+            return ei
+
+        def e_quantize(g, ei):
+            flat = ei[:].rearrange("p c t -> p (c t)")
+            nc.vector.quantize_mx(out=ec[:, g, 0:1024].bitcast(E4M3), scales=es[:, g, 0:1024], in_=flat[:, 0:4096])
+            nc.vector.quantize_mx(
+                out=ec[:, g, 1024:1536].bitcast(E4M3), scales=es[:, g, 1024:1536], in_=flat[:, 4096:6144]
+            )
+
+        def words(t):
+            return t.bitcast(F32)
+
+        def turn(srcs, dst, eng):
+            n = len(srcs)
+            tp = ps.tile([P, 2, 2, 128], F32, name="tp", tag="tp", bufs=2)
+            for i in range(n):
+                for u in range(2):
+                    nc.tensor.transpose(tp[:, i, u, :], srcs[i][:, u:256:2], ident[:])
+            dv = dst.bitcast(F32).rearrange("p (a r u) -> p a r u", a=n, u=2)
+            sv = tp[:, 0:n].rearrange("p a u r -> p a r u")
+            if eng == 0:
+                nc.vector.tensor_copy(out=dv, in_=sv)
+            else:
+                nc.scalar.copy(out=dv, in_=sv)
+
+        def out1_block(mi):
+            o1 = sb.tile([P, 1536], F32, name="o1", tag="o1")
+            for n in range(3):
+                a1 = ps.tile([P, 512], F32, name="a1", tag="a1", bufs=2)
+                for g in range(2):
+                    nc.tensor.matmul_mx(
+                        out=a1[:],
+                        lhsT=d3c[:, g, 128 * mi:128 * (mi + 1)].bitcast(E5M2),
+                        lhsT_scale=d3s[:, g, 128 * mi:128 * (mi + 1)],
+                        rhs=ec[:, g, 512 * n:512 * (n + 1)].bitcast(E4M3), rhs_scale=es[:, g, 512 * n:512 * (n + 1)],
+                        start=(g == 0), stop=(g == 1),
+                    )
+                nc.scalar.copy(out=o1[:, 512 * n:512 * (n + 1)], in_=a1[:])
+            nc.scalar.dma_start(out=o1_v[:, mi, :], in_=o1[:])
+
+        ident = sb.tile([P, P], F32, name="ident", tag="ident")
+        make_identity(nc, ident[:])
+        c15 = sb.tile([P, P], BF16, name="c15", tag="c15")
+        nc.vector.tensor_scalar_mul(out=c15[:], in0=ident[:], scalar1=1.5)
+        mhalf = sb.tile([P, P], BF16, name="mhalf", tag="mhalf")
+        nc.vector.tensor_scalar_mul(out=mhalf[:], in0=ident[:], scalar1=-0.5)
+        ones = sb.tile([P, 512], BF16, name="ones", tag="ones")
+        nc.vector.memset(ones[:], 1.0)
+
+        first = []
+        todo = []
+        units = {}
+        grs = {}
+        d3t = {}
+        o_tiles = {}
+
+        def fill():
+            if len(first) > 0:
+                first.pop(0)()
+            elif len(todo) > 0:
+                todo.pop(0)()
+
+        units[0] = unit_tiles()
+        load_part(units[0], 0, 0, 512)
+        w12 = sb.tile([P, 4, 1536], BF16, name="w12", tag="big", bufs=2, align_bytes=64)
+        nc.sync.dma_start(out=w12[:, :, 0:512], in_=w1_v)
+        graw0 = load_g(0)
+        nc.sync.dma_start(out=w12[:, :, 512:1536], in_=w2_v)
+        load_part(units[0], 0, 512, 1024)
+        z30 = load_z3(0)
+        w3r = sb.tile([P, 4, 1536], BF16, name="w3r", tag="big", bufs=2, align_bytes=64)
+        nc.sync.dma_start(out=w3r[:], in_=w3_v)
+        units[1] = unit_tiles()
+        load_part(units[1], 1, 0, 1024)
+
+        w_src = [w12[:, :, 0:512].rearrange("p t (c d) -> p c d t", d=32)]
+        for a in range(2):
+            w_src.append(w12[:, :, 512:1536].rearrange("p t (c a d) -> p a c d t", a=2, d=32)[:, a])
+        for a in range(3):
+            w_src.append(w3r[:].rearrange("p t (c a d) -> p a c d t", a=3, d=32)[:, a])
+
+        def w_step(b, il):
+            def go():
+                w_quantize(b, il)
+                if b + 2 < 6:
+                    first.append(w_step(b + 2, w_interleave(w_src[b + 2])))
+            return go
+
+        for b in range(2):
+            first.append(w_step(b, w_interleave(w_src[b])))
+
+        def height3(g, z3):
+            d3 = sb.tile([P, 4, 512], BF16, name="d3", tag="d3")
+            for j in range(4):
+                nc.vector.scalar_tensor_tensor(
+                    out=d3[:, j, :], in0=z3[:, j, :], scalar=0.0, in1=grs[(g, j)][:, :, 2],
+                    op0=ALU.is_gt, op1=ALU.mult,
+                )
+            d3w = d3[:].rearrange("p j f -> p (j f)").bitcast(F32)
+            g3 = sb.tile([P, 2048], BF16, name="g3", tag="hil", bufs=2, align_bytes=64)
+            for x in range(2):
+                turn([d3w[:, 512 * x:512 * x + 256], d3w[:, 512 * x + 256:512 * x + 512]],
+                     g3[:, 1024 * x:1024 * (x + 1)], 1)
+            i3 = sb.tile([P, 2048], BF16, name="i3", tag="hil", bufs=2, align_bytes=64)
+            nc.scalar.copy(out=i3[:].rearrange("p (c t) -> p c t", t=4), in_=d3[:].rearrange("p t c -> p c t"))
+
+            def q_t():
+                nc.vector.quantize_mx(out=t3c[:, g, :].bitcast(E5M2), scales=t3s[:, g, :], in_=g3[:])
+
+            def q_i():
+                nc.vector.quantize_mx(out=d3c[:, g, :].bitcast(E5M2), scales=d3s[:, g, :], in_=i3[:])
+
+            first.append(q_t)
+            first.append(q_i)
+
+        def mx(acc, lc, lsc, b, start, stop):
+            nc.tensor.matmul_mx(
+                out=acc[:], lhsT=lc.bitcast(E5M2), lhsT_scale=lsc,
+                rhs=wc[:, b, :].bitcast(E4M3), rhs_scale=ws[:, b, :], start=start, stop=stop,
+            )
+
+        def finish(r, grp):
+            u, jj = divmod(r, 2)
+            g, jp = divmod(u, 2)
+            j = r % 4
+            st = {}
+
+            def col(a):
+                return st["dc"][:, 128 * a:128 * (a + 1)], st["ds"][:, 128 * a:128 * (a + 1)]
+
+            def q0():
+                dc = sb.tile([P, 640], U32, name="dc", tag="dc", bufs=3, align_bytes=64)
+                dsc = sb.tile([P, 640], U8, name="dsc", tag="dsc", bufs=3, align_bytes=64)
+                st["dc"] = dc
+                st["ds"] = dsc
+                nc.vector.quantize_mx(out=dc[:, 0:256].bitcast(E5M2), scales=dsc[:, 0:256], in_=grp[:, 0:1024])
+                acc = []
+                for l in range(3):
+                    acc_l = ps.tile([P, 512], F32, name="acc%d" % l, tag="acc%d" % l)
+                    acc.append(acc_l)
+                    mx(acc_l, t3c[:, g, 128 * j:128 * (j + 1)], t3s[:, g, 128 * j:128 * (j + 1)], 3 + l, True, False)
+                st["acc"] = acc
+                for a, b, l in ((0, 1, 0), (0, 2, 1), (1, 1, 1), (1, 2, 2)):
+                    lc, lsc = col(a)
+                    mx(acc[l], lc, lsc, b, False, False)
+
+            def q1():
+                nc.vector.quantize_mx(
+                    out=st["dc"][:, 256:512].bitcast(E5M2), scales=st["ds"][:, 256:512], in_=grp[:, 1024:2048]
+                )
+
+            def q2():
+                nc.vector.quantize_mx(
+                    out=st["dc"][:, 512:640].bitcast(E5M2), scales=st["ds"][:, 512:640], in_=grp[:, 2048:2560]
+                )
+                if jj == 0:
+                    o_new = sb.tile([P, 16, 2, 96], F32, name="o", tag="o", bufs=2)
+                    o_tiles[u] = o_new
+                o = o_tiles[u]
+                for l in range(3):
+                    lc, lsc = col(2 + l)
+                    mx(st["acc"][l], lc, lsc, 0, False, True)
+                for l in range(3):
+                    dst = o[:, :, jj, 32 * l:32 * (l + 1)]
+                    src = st["acc"][l][:].rearrange("p (c d) -> p c d", d=32)
+                    if r == 7 and l == 1:
+                        nc.vector.tensor_copy(out=dst, in_=src)
+                    else:
+                        nc.scalar.copy(out=dst, in_=src)
+                if u == 3:
+                    nc.scalar.dma_start(
+                        out=o0_v[g][:, :, 192 * jp + 96 * jj:192 * jp + 96 * (jj + 1)], in_=o[:, :, jj, :]
+                    )
+                elif jj == 1:
+                    nc.scalar.dma_start(
+                        out=o0_v[g][:, :, 192 * jp:192 * (jp + 1)], in_=o[:].rearrange("p c j w -> p c (j w)")
+                    )
+
+            return [q0, q1, q2]
+
+        def row(r):
+            u, jj = divmod(r, 2)
+            g = u // 2
+            j = r % 4
+            z1, z2 = units[u]
+            sl = slice(512 * jj, 512 * (jj + 1))
+            dz = sb.tile([P, 5, 512], BF16, name="dz", tag="dz", bufs=2)
+            m = sb.tile([P, 512], F32, name="m", tag="m")
+            t2 = sb.tile([P, 512], BF16, name="t2", tag="t2")
+            gn1 = sb.tile([P, 512], BF16, name="gn1", tag="gn1")
+            gn2 = sb.tile([P, 512], BF16, name="gn2", tag="gn2")
+            nc.vector.tensor_tensor(out=m[:], in0=z1[:, 0, sl], in1=z1[:, 1, sl], op=ALU.max)
+            nc.vector.scalar_tensor_tensor(
+                out=dz[:, 0, :], in0=z2[:, 1, sl], scalar=TINY, in1=z2[:, 0, sl], op0=ALU.max, op1=ALU.is_le
+            )
+            nc.vector.scalar_tensor_tensor(
+                out=m[:], in0=z1[:, 2, sl], scalar=TINY, in1=m[:], op0=ALU.max, op1=ALU.max
+            )
+            nc.vector.scalar_tensor_tensor(
+                out=dz[:, 1, :], in0=z2[:, 0, sl], scalar=TINY, in1=z2[:, 1, sl], op0=ALU.max, op1=ALU.is_le
+            )
+            nc.vector.tensor_tensor(
+                out=dz[:, 2:5, :], in0=z1[:, :, sl], in1=m[:].unsqueeze(1).to_broadcast([P, 3, 512]), op=ALU.is_ge
+            )
+            cnt = ps.tile([P, 512], F32, name="cnt", tag="cnt")
+            nc.tensor.matmul(out=cnt[:], lhsT=c15[:], rhs=ones[:], start=True, stop=False)
+            for q in range(3):
+                nc.tensor.matmul(out=cnt[:], lhsT=mhalf[:], rhs=dz[:, 2 + q, :], start=False, stop=(q == 2))
+            if r > 0:
+                fill()
+            nc.vector.tensor_tensor(out=t2[:], in0=dz[:, 0, :], in1=dz[:, 1, :], op=ALU.mult)
+            if r > 0:
+                fill()
+            nc.vector.tensor_scalar(out=t2[:], in0=t2[:], scalar1=-0.5, scalar2=1.0, op0=ALU.mult, op1=ALU.add)
+            if r > 0:
+                fill()
+            if r == 0:
+                for jx in range(4):
+                    grs[(0, jx)] = reorder_g(graw0, jx, jx % 2)
+            nc.vector.tensor_tensor(out=gn2[:], in0=t2[:], in1=grs[(g, j)][:, :, 1], op=ALU.mult)
+            if r > 0:
+                fill()
+            nc.vector.scalar_tensor_tensor(
+                out=gn1[:], in0=cnt[:], scalar=THIRD, in1=grs[(g, j)][:, :, 0], op0=ALU.max, op1=ALU.mult
+            )
+            nc.vector.tensor_tensor(
+                out=dz[:, 0:2, :], in0=dz[:, 0:2, :], in1=gn2[:].unsqueeze(1).to_broadcast([P, 2, 512]), op=ALU.mult
+            )
+            dzw = dz[:].rearrange("p a f -> p (a f)").bitcast(F32)
+            grp = sb.tile([P, 2560], BF16, name="grp", tag="grp", bufs=3, align_bytes=64)
+            turn([dzw[:, 0:256], dzw[:, 256:512]], grp[:, 0:1024], 1)
+            if r > 0:
+                fill()
+            nc.vector.tensor_tensor(
+                out=dz[:, 2:5, :], in0=dz[:, 2:5, :], in1=gn1[:].unsqueeze(1).to_broadcast([P, 3, 512]), op=ALU.mult
+            )
+            turn([dzw[:, 512:768], dzw[:, 768:1024]], grp[:, 1024:2048], 1)
+            turn([dzw[:, 1024:1280]], grp[:, 2048:2560], 0 if r == 7 else 1)
+            if r > 0:
+                fill()
+            todo.extend(finish(r, grp))
+
+        eraws = {}
+        for r in range(8):
+            row(r)
+            if r == 0:
+                height3(0, z30)
+                eraws[0] = e_load(0)
+                graw1 = load_g(1)
+                z31 = load_z3(1)
+            if r == 1:
+                units[2] = unit_tiles()
+                load_part(units[2], 2, 0, 1024)
+                for jx in range(2):
+                    grs[(1, jx)] = reorder_g(graw1, jx, 1)
+            if r == 2:
+                ei0 = e_interleave(eraws[0])
+                first.append(lambda: e_quantize(0, ei0))
+                eraws[1] = e_load(1)
+                grs[(1, 2)] = reorder_g(graw1, 2, 0)
+            if r == 3:
+                units[3] = unit_tiles()
+                load_part(units[3], 3, 0, 1024)
+                grs[(1, 3)] = reorder_g(graw1, 3, 0)
+                height3(1, z31)
+                ei1 = e_interleave(eraws[1])
+                first.append(lambda: e_quantize(1, ei1))
+            if r == 4:
+                out1_block(0)
+                out1_block(1)
+            if r == 5:
+                out1_block(2)
+                out1_block(3)
+        for k in range(len(first) + len(todo)):
+            fill()

@@ -127,7 +127,7 @@ def tile_vrtconv_t_v_kernel(tc, Ec, W1, W2, W3, b1, b2, b3, conv1, conv2, conv3,
                 nc.scalar.copy(out=dv, in_=sv)
 
         def out1_block(mi):
-            o1 = sb.tile([P, 1536], F32, name="o1", tag="o1")
+            o1 = sb.tile([P, 1536], F32, name="o1", tag=("o1", "z3", "graw", "o1")[mi])
             for n in range(3):
                 a1 = ps.tile([P, 512], F32, name="a1", tag="a1", bufs=2)
                 for g in range(2):

@@ -319,7 +319,7 @@ def tile_vrtconv_t_v_kernel(tc, Ec, W1, W2, W3, b1, b2, b3, conv1, conv2, conv3,
                 fill()
             if r == 0:
                 for jx in range(4):
-                    grs[(0, jx)] = reorder_g(graw0, jx, jx % 2)
+                    grs[(0, jx)] = reorder_g(graw0, jx, 0)
             nc.vector.tensor_tensor(out=gn2[:], in0=t2[:], in1=grs[(g, j)][:, :, 1], op=ALU.mult)
             if r > 0:
                 fill()
@@ -355,7 +355,7 @@ def tile_vrtconv_t_v_kernel(tc, Ec, W1, W2, W3, b1, b2, b3, conv1, conv2, conv3,
                 units[2] = unit_tiles()
                 load_part(units[2], 2, 0, 1024)
                 for jx in range(2):
-                    grs[(1, jx)] = reorder_g(graw1, jx, 1)
+                    grs[(1, jx)] = reorder_g(graw1, jx, 0)
             if r == 2:
                 ei0 = e_interleave(eraws[0])
                 first.append(lambda: e_quantize(0, ei0))

from contextlib import ExitStack

import concourse.mybir as mybir
from concourse.masks import make_identity

FLOPS = 6979321856

F32 = mybir.dt.float32
BF16 = mybir.dt.bfloat16
U32 = mybir.dt.uint32
U8 = mybir.dt.uint8
E4M3 = mybir.dt.float8_e4m3fn_x4
E5M2 = mybir.dt.float8_e5m2_x4
ALU = mybir.AluOpType

P = 128
TINY = 1e-45
THIRD = 1.0 / 3.0


def tile_vrtconv_t_v_kernel(tc, Ec, W1, W2, W3, b1, b2, b3, conv1, conv2, conv3, grad_out, out_0, out_1):
    nc = tc.nc

    g_v = grad_out.rearrange("o (g p j) x i -> g p o (j x i)", g=2, p=P, j=4)
    e_v = Ec.rearrange("c (g p j) l d -> g p c (j l d)", g=2, p=P, j=4)
    z1_v = conv1.rearrange("q (g p j) k o -> g p q (j k o)", g=2, p=P, j=4)
    z2_v = conv2.rearrange("q (g p j) k o -> g p q (j k o)", g=2, p=P, j=4)
    z3_v = conv3.rearrange("q (g p j) k o -> g p (q j k o)", g=2, p=P, j=4)
    w1_v = W1.rearrange("k o c a d -> (k o) (c a d)").rearrange("(p t) w -> p t w", t=4)
    w2_v = W2.rearrange("k o c a d -> (k o) (c a d)").rearrange("(p t) w -> p t w", t=4)
    w3_v = W3.rearrange("k o c a d -> (k o) (c a d)").rearrange("(p t) w -> p t w", t=4)
    o0_v = out_0.rearrange("c (g p j) l d -> g p c (j l d)", g=2, p=P, j=4)
    o1_v = out_1.rearrange("k o c a d -> (k o) (c a d)").rearrange("(m p) w -> p m w", p=P)

    with ExitStack() as ctx:
        sb = ctx.enter_context(tc.tile_pool(name="sb", bufs=1))
        ps = ctx.enter_context(tc.psum_pool(name="ps", bufs=1))

        wc = sb.tile([P, 6, 512], U32, name="wc", tag="wc", align_bytes=64)
        ws = sb.tile([P, 6, 512], U8, name="ws", tag="ws", align_bytes=64)
        ec = sb.tile([P, 2, 1536], U32, name="ec", tag="ec", align_bytes=64)
        es = sb.tile([P, 2, 1536], U8, name="es", tag="es", align_bytes=64)
        d3c = sb.tile([P, 2, 512], U32, name="d3c", tag="d3c", align_bytes=64)
        d3s = sb.tile([P, 2, 512], U8, name="d3s", tag="d3s", align_bytes=64)
        t3c = sb.tile([P, 2, 512], U32, name="t3c", tag="t3c", align_bytes=64)
        t3s = sb.tile([P, 2, 512], U8, name="t3s", tag="t3s", align_bytes=64)

        def load_g(g):
            graw = sb.tile([P, 16, 384], BF16, name="graw", tag="graw")
            nc.sync.dma_start(out=graw[:], in_=g_v[g])
            return graw

        def load_z3(g):
            z3 = sb.tile([P, 4, 512], F32, name="z3", tag="z3")
            nc.sync.dma_start(out=z3[:].rearrange("p j f -> p (j f)"), in_=z3_v[g])
            return z3

        def unit_tiles():
            z1 = sb.tile([P, 3, 1024], F32, name="z1", tag="z1", bufs=2)
            z2 = sb.tile([P, 2, 1024], F32, name="z2", tag="z2", bufs=2)
            return z1, z2

        def load_part(zz, u, lo, hi):
            g, jp = divmod(u, 2)
            nc.sync.dma_start(out=zz[0][:, :, lo:hi], in_=z1_v[g][:, :, 1024 * jp + lo:1024 * jp + hi])
            nc.sync.dma_start(out=zz[1][:, :, lo:hi], in_=z2_v[g][:, :, 1024 * jp + lo:1024 * jp + hi])

        def reorder_g(graw, j, eng):
            gr = sb.tile([P, 512, 3], BF16, name="gr", tag="gr", bufs=4)
            dst = gr[:].rearrange("p (k o) h -> p k o h", o=16)
            src = graw[:, :, 96 * j:96 * (j + 1)].rearrange("p o (k h) -> p k o h", h=3)
            if eng == 0:
                nc.vector.tensor_copy(out=dst, in_=src)
            else:
                nc.scalar.copy(out=dst, in_=src)
            return gr

        def il_tile():
            il = sb.tile([P, 512, 4], BF16, name="il", tag="il", bufs=2, align_bytes=64)
            return il

        def w_interleave(src):
            il = il_tile()
            nc.scalar.copy(out=il[:].rearrange("p (c d) t -> p c d t", d=32), in_=src)
            return il

        def w_quantize(b, il):
            nc.vector.quantize_mx(
                out=wc[:, b, :].bitcast(E4M3), scales=ws[:, b, :], in_=il[:].rearrange("p c t -> p (c t)")
            )

        def e_load(g):
            eraw = sb.tile([P, 16, 384], BF16, name="eraw", tag="big", bufs=2, align_bytes=64)
            nc.sync.dma_start(out=eraw[:], in_=e_v[g])
            return eraw

        def e_interleave(eraw):
            ei = sb.tile([P, 1536, 4], BF16, name="ei", tag="big", bufs=2, align_bytes=64)
            for i in range(4):
                nc.scalar.copy(
                    out=ei[:, 384 * i:384 * (i + 1), :].rearrange("p (c w) t -> p c w t", w=96),
                    in_=eraw[:, 4 * i:4 * i + 4, :].rearrange("p c (t w) -> p c w t", t=4),
                )
            return ei

        def e_quantize(g, ei):
            flat = ei[:].rearrange("p c t -> p (c t)")
            nc.vector.quantize_mx(out=ec[:, g, 0:1024].bitcast(E4M3), scales=es[:, g, 0:1024], in_=flat[:, 0:4096])
            nc.vector.quantize_mx(
                out=ec[:, g, 1024:1536].bitcast(E4M3), scales=es[:, g, 1024:1536], in_=flat[:, 4096:6144]
            )

        def words(t):
            return t.bitcast(F32)

        def turn(srcs, dst, eng):
            n = len(srcs)
            tp = ps.tile([P, 2, 2, 128], F32, name="tp", tag="tp", bufs=2)
            for i in range(n):
                for u in range(2):
                    nc.tensor.transpose(tp[:, i, u, :], srcs[i][:, u:256:2], ident[:])
            dv = dst.bitcast(F32).rearrange("p (a r u) -> p a r u", a=n, u=2)
            sv = tp[:, 0:n].rearrange("p a u r -> p a r u")
            if eng == 0:
                nc.vector.tensor_copy(out=dv, in_=sv)
            else:
                nc.scalar.copy(out=dv, in_=sv)

        def out1_block(mi):
            o1 = sb.tile([P, 1536], F32, name="o1", tag=("o1", "z3", "graw", "o1")[mi])
            for n in range(3):
                a1 = ps.tile([P, 512], F32, name="a1", tag="a1", bufs=2)
                for g in range(2):
                    nc.tensor.matmul_mx(
                        out=a1[:],
                        lhsT=d3c[:, g, 128 * mi:128 * (mi + 1)].bitcast(E5M2),
                        lhsT_scale=d3s[:, g, 128 * mi:128 * (mi + 1)],
                        rhs=ec[:, g, 512 * n:512 * (n + 1)].bitcast(E4M3), rhs_scale=es[:, g, 512 * n:512 * (n + 1)],
                        start=(g == 0), stop=(g == 1),
                    )
                nc.scalar.copy(out=o1[:, 512 * n:512 * (n + 1)], in_=a1[:])
            nc.scalar.dma_start(out=o1_v[:, mi, :], in_=o1[:])

        ident = sb.tile([P, P], F32, name="ident", tag="ident")
        make_identity(nc, ident[:])
        c15 = sb.tile([P, P], BF16, name="c15", tag="c15")
        nc.vector.tensor_scalar_mul(out=c15[:], in0=ident[:], scalar1=1.5)
        mhalf = sb.tile([P, P], BF16, name="mhalf", tag="mhalf")
        nc.vector.tensor_scalar_mul(out=mhalf[:], in0=ident[:], scalar1=-0.5)
        ones = sb.tile([P, 512], BF16, name="ones", tag="ones")
        nc.vector.memset(ones[:], 1.0)

        first = []
        todo = []
        units = {}
        grs = {}
        d3t = {}
        o_tiles = {}

        def fill():
            if len(first) > 0:
                first.pop(0)()
            elif len(todo) > 0:
                todo.pop(0)()

        units[0] = unit_tiles()
        load_part(units[0], 0, 0, 512)
        w12 = sb.tile([P, 4, 1536], BF16, name="w12", tag="big", bufs=2, align_bytes=64)
        nc.sync.dma_start(out=w12[:, :, 0:512], in_=w1_v)
        graw0 = load_g(0)
        nc.sync.dma_start(out=w12[:, :, 512:1536], in_=w2_v)
        load_part(units[0], 0, 512, 1024)
        z30 = load_z3(0)
        w3r = sb.tile([P, 4, 1536], BF16, name="w3r", tag="big", bufs=2, align_bytes=64)
        nc.sync.dma_start(out=w3r[:], in_=w3_v)
        units[1] = unit_tiles()
        load_part(units[1], 1, 0, 1024)

        w_src = [w12[:, :, 0:512].rearrange("p t (c d) -> p c d t", d=32)]
        for a in range(2):
            w_src.append(w12[:, :, 512:1536].rearrange("p t (c a d) -> p a c d t", a=2, d=32)[:, a])
        for a in range(3):
            w_src.append(w3r[:].rearrange("p t (c a d) -> p a c d t", a=3, d=32)[:, a])

        def w_step(b, il):
            def go():
                w_quantize(b, il)
                if b + 2 < 6:
                    first.append(w_step(b + 2, w_interleave(w_src[b + 2])))
            return go

        for b in range(2):
            first.append(w_step(b, w_interleave(w_src[b])))

        def height3(g, z3):
            d3 = sb.tile([P, 4, 512], BF16, name="d3", tag="d3")
            for j in range(4):
                nc.vector.scalar_tensor_tensor(
                    out=d3[:, j, :], in0=z3[:, j, :], scalar=0.0, in1=grs[(g, j)][:, :, 2],
                    op0=ALU.is_gt, op1=ALU.mult,
                )
            d3w = d3[:].rearrange("p j f -> p (j f)").bitcast(F32)
            g3 = sb.tile([P, 2048], BF16, name="g3", tag="hil", bufs=2, align_bytes=64)
            for x in range(2):
                turn([d3w[:, 512 * x:512 * x + 256], d3w[:, 512 * x + 256:512 * x + 512]],
                     g3[:, 1024 * x:1024 * (x + 1)], 1)
            i3 = sb.tile([P, 2048], BF16, name="i3", tag="hil", bufs=2, align_bytes=64)
            nc.scalar.copy(out=i3[:].rearrange("p (c t) -> p c t", t=4), in_=d3[:].rearrange("p t c -> p c t"))

            def q_t():
                nc.vector.quantize_mx(out=t3c[:, g, :].bitcast(E5M2), scales=t3s[:, g, :], in_=g3[:])

            def q_i():
                nc.vector.quantize_mx(out=d3c[:, g, :].bitcast(E5M2), scales=d3s[:, g, :], in_=i3[:])

            first.append(q_t)
            first.append(q_i)

        def mx(acc, lc, lsc, b, start, stop):
            nc.tensor.matmul_mx(
                out=acc[:], lhsT=lc.bitcast(E5M2), lhsT_scale=lsc,
                rhs=wc[:, b, :].bitcast(E4M3), rhs_scale=ws[:, b, :], start=start, stop=stop,
            )

        def finish(r, grp):
            u, jj = divmod(r, 2)
            g, jp = divmod(u, 2)
            j = r % 4
            st = {}

            def col(a):
                return st["dc"][:, 128 * a:128 * (a + 1)], st["ds"][:, 128 * a:128 * (a + 1)]

            def q0():
                dc = sb.tile([P, 640], U32, name="dc", tag="dc", bufs=3, align_bytes=64)
                dsc = sb.tile([P, 640], U8, name="dsc", tag="dsc", bufs=3, align_bytes=64)
                st["dc"] = dc
                st["ds"] = dsc
                nc.vector.quantize_mx(out=dc[:, 0:256].bitcast(E5M2), scales=dsc[:, 0:256], in_=grp[:, 0:1024])
                acc = []
                for l in range(3):
                    acc_l = ps.tile([P, 512], F32, name="acc%d" % l, tag="acc%d" % l)
                    acc.append(acc_l)
                    mx(acc_l, t3c[:, g, 128 * j:128 * (j + 1)], t3s[:, g, 128 * j:128 * (j + 1)], 3 + l, True, False)
                st["acc"] = acc
                for a, b, l in ((0, 1, 0), (0, 2, 1), (1, 1, 1), (1, 2, 2)):
                    lc, lsc = col(a)
                    mx(acc[l], lc, lsc, b, False, False)

            def q1():
                nc.vector.quantize_mx(
                    out=st["dc"][:, 256:512].bitcast(E5M2), scales=st["ds"][:, 256:512], in_=grp[:, 1024:2048]
                )

            def q2():
                nc.vector.quantize_mx(
                    out=st["dc"][:, 512:640].bitcast(E5M2), scales=st["ds"][:, 512:640], in_=grp[:, 2048:2560]
                )
                if jj == 0:
                    o_new = sb.tile([P, 16, 2, 96], F32, name="o", tag="o", bufs=2)
                    o_tiles[u] = o_new
                o = o_tiles[u]
                for l in range(3):
                    lc, lsc = col(2 + l)
                    mx(st["acc"][l], lc, lsc, 0, False, True)
                for l in range(3):
                    dst = o[:, :, jj, 32 * l:32 * (l + 1)]
                    src = st["acc"][l][:].rearrange("p (c d) -> p c d", d=32)
                    if r == 7 and l == 1:
                        nc.vector.tensor_copy(out=dst, in_=src)
                    else:
                        nc.scalar.copy(out=dst, in_=src)
                if u == 3:
                    nc.scalar.dma_start(
                        out=o0_v[g][:, :, 192 * jp + 96 * jj:192 * jp + 96 * (jj + 1)], in_=o[:, :, jj, :]
                    )
                elif jj == 1:
                    nc.scalar.dma_start(
                        out=o0_v[g][:, :, 192 * jp:192 * (jp + 1)], in_=o[:].rearrange("p c j w -> p c (j w)")
                    )

            return [q0, q1, q2]

        def row(r):
            u, jj = divmod(r, 2)
            g = u // 2
            j = r % 4
            z1, z2 = units[u]
            sl = slice(512 * jj, 512 * (jj + 1))
            dz = sb.tile([P, 5, 512], BF16, name="dz", tag="dz", bufs=2)
            m = sb.tile([P, 512], F32, name="m", tag="m")
            t2 = sb.tile([P, 512], BF16, name="t2", tag="t2")
            gn1 = sb.tile([P, 512], BF16, name="gn1", tag="gn1")
            gn2 = sb.tile([P, 512], BF16, name="gn2", tag="gn2")
            nc.vector.tensor_tensor(out=m[:], in0=z1[:, 0, sl], in1=z1[:, 1, sl], op=ALU.max)
            nc.vector.scalar_tensor_tensor(
                out=dz[:, 0, :], in0=z2[:, 1, sl], scalar=TINY, in1=z2[:, 0, sl], op0=ALU.max, op1=ALU.is_le
            )
            nc.vector.scalar_tensor_tensor(
                out=m[:], in0=z1[:, 2, sl], scalar=TINY, in1=m[:], op0=ALU.max, op1=ALU.max
            )
            nc.vector.scalar_tensor_tensor(
                out=dz[:, 1, :], in0=z2[:, 0, sl], scalar=TINY, in1=z2[:, 1, sl], op0=ALU.max, op1=ALU.is_le
            )
            nc.vector.tensor_tensor(
                out=dz[:, 2:5, :], in0=z1[:, :, sl], in1=m[:].unsqueeze(1).to_broadcast([P, 3, 512]), op=ALU.is_ge
            )
            cnt = ps.tile([P, 512], F32, name="cnt", tag="cnt")
            nc.tensor.matmul(out=cnt[:], lhsT=c15[:], rhs=ones[:], start=True, stop=False)
            for q in range(3):
                nc.tensor.matmul(out=cnt[:], lhsT=mhalf[:], rhs=dz[:, 2 + q, :], start=False, stop=(q == 2))
            if r > 0:
                fill()
            nc.vector.tensor_tensor(out=t2[:], in0=dz[:, 0, :], in1=dz[:, 1, :], op=ALU.mult)
            if r > 0:
                fill()
            nc.vector.tensor_scalar(out=t2[:], in0=t2[:], scalar1=-0.5, scalar2=1.0, op0=ALU.mult, op1=ALU.add)
            if r > 0:
                fill()
            if r == 0:
                for jx in range(4):
                    grs[(0, jx)] = reorder_g(graw0, jx, 0)
            nc.vector.tensor_tensor(out=gn2[:], in0=t2[:], in1=grs[(g, j)][:, :, 1], op=ALU.mult)
            if r > 0:
                fill()
            nc.vector.scalar_tensor_tensor(
                out=gn1[:], in0=cnt[:], scalar=THIRD, in1=grs[(g, j)][:, :, 0], op0=ALU.max, op1=ALU.mult
            )
            nc.vector.tensor_tensor(
                out=dz[:, 0:2, :], in0=dz[:, 0:2, :], in1=gn2[:].unsqueeze(1).to_broadcast([P, 2, 512]), op=ALU.mult
            )
            dzw = dz[:].rearrange("p a f -> p (a f)").bitcast(F32)
            grp = sb.tile([P, 2560], BF16, name="grp", tag="grp", bufs=3, align_bytes=64)
            turn([dzw[:, 0:256], dzw[:, 256:512]], grp[:, 0:1024], 1)
            if r > 0:
                fill()
            nc.vector.tensor_tensor(
                out=dz[:, 2:5, :], in0=dz[:, 2:5, :], in1=gn1[:].unsqueeze(1).to_broadcast([P, 3, 512]), op=ALU.mult
            )
            turn([dzw[:, 512:768], dzw[:, 768:1024]], grp[:, 1024:2048], 1)
            turn([dzw[:, 1024:1280]], grp[:, 2048:2560], 0 if r == 7 else 1)
            if r > 0:
                fill()
            todo.extend(finish(r, grp))

        eraws = {}
        for r in range(8):
            row(r)
            if r == 0:
                height3(0, z30)
                eraws[0] = e_load(0)
                graw1 = load_g(1)
                z31 = load_z3(1)
            if r == 1:
                units[2] = unit_tiles()
                load_part(units[2], 2, 0, 1024)
                for jx in range(2):
                    grs[(1, jx)] = reorder_g(graw1, jx, 0)
            if r == 2:
                ei0 = e_interleave(eraws[0])
                first.append(lambda: e_quantize(0, ei0))
                eraws[1] = e_load(1)
                grs[(1, 2)] = reorder_g(graw1, 2, 0)
            if r == 3:
                units[3] = unit_tiles()
                load_part(units[3], 3, 0, 1024)
                grs[(1, 3)] = reorder_g(graw1, 3, 0)
                height3(1, z31)
                ei1 = e_interleave(eraws[1])
                first.append(lambda: e_quantize(1, ei1))
            if r == 4:
                out1_block(0)
                out1_block(1)
            if r == 5:
                out1_block(2)
                out1_block(3)
        for k in range(len(first) + len(todo)):
            fill()
